import numpy as np
import ml_dtypes


def mxq(x, axis, fmt="e4m3"):
    dtype, down = {"e4m3": (ml_dtypes.float8_e4m3fn, 7), "e5m2": (ml_dtypes.float8_e5m2, 14)}[fmt]
    v = np.moveaxis(np.asarray(x, np.float32).astype(ml_dtypes.bfloat16).astype(np.float64), axis, -1)
    blocks = v.reshape(v.shape[:-1] + (-1, 32))
    amax = np.abs(blocks).max(-1, keepdims=True)
    byte = np.maximum(np.where(amax > 0, np.frexp(amax)[1] - 1 + 127, 0) - down, 1)
    scale = np.exp2(byte - 127.0)
    codes = (blocks / scale).astype(np.float32).astype(dtype).astype(np.float64)
    return np.moveaxis((codes * scale).reshape(v.shape), -1, axis)


WIDE = False


def mx_kscale(k):
    if not WIDE:
        return np.ones(k)
    levels = np.array([10, -10, 5, -5, 0])
    if k % 512:
        return np.exp2(np.random.permutation(np.resize(levels, k // 32))).repeat(32)
    a = np.empty((k // 512, 16))
    for p in range(k // 512):
        a[p, :8] = np.random.permutation(np.resize(levels, 8))
        for g in range(8):
            far = levels[np.abs(levels - a[p, g]) >= 10]
            a[p, g + 8] = far[np.random.randint(len(far))]
    return np.exp2(a.ravel()).repeat(32)


BF16 = ml_dtypes.bfloat16


def bf(x):
    return np.asarray(x, np.float32).astype(BF16)


def f64(x):
    return np.asarray(x).astype(np.float64)


B, T, C, HS, DW, DA, DV, DG = 4, 1024, 1024, 64, 128, 128, 128, 256


def sigmoid(z):
    return 1.0 / (1.0 + np.exp(-z))


def setup_inputs():
    s = mx_kscale(C)
    return {
        "x": bf(np.random.standard_normal((B, T, C)) * s),
        "v_first": bf(np.random.standard_normal((B, T, C))),
        "x_v": bf(np.random.uniform(0.0, 1.0, C)),
        "Wv": bf(np.random.standard_normal((C, C)) / np.sqrt(C) / s[None, :]),
        "v0": bf(np.random.standard_normal(C)),
        "xv_v1": bf(0.8 * np.random.standard_normal((B, T, DV))),
        "v2": bf(np.random.standard_normal((DV, C)) / np.sqrt(DV)),
    }


def reference(x, v_first, x_v, Wv, v0, xv_v1, v2):
    x = f64(x)
    xprev = np.concatenate([np.zeros_like(x[:, :1]), x[:, :-1]], axis=1)
    xx = xprev - x
    xv = x + xx * f64(x_v)
    v = mxq(xv, 2, "e4m3") @ mxq(f64(Wv), 1, "e4m3").T
    v = v + (f64(v_first) - v) * sigmoid(f64(v0) + f64(xv_v1) @ f64(v2))
    return v

@@ -1,0 +1,353 @@
+from contextlib import ExitStack
+
+import concourse.mybir as mybir
+from concourse.masks import make_identity
+
+F32 = mybir.dt.float32
+BF16 = mybir.dt.bfloat16
+U32 = mybir.dt.uint32
+U8 = mybir.dt.uint8
+FP8X4 = mybir.dt.float8_e4m3fn_x4
+ALU = mybir.AluOpType
+ACT = mybir.ActivationFunctionType
+
+P = 128
+TOK = 4096
+C = 1024
+DV = 128
+CHUNK = 512
+NCHUNK = TOK // CHUNK
+NT = TOK // P
+SEQ_CHUNKS = 1024 // CHUNK
+TW = CHUNK + 4
+HALF = CHUNK // 2
+
+FLOPS = 2 * TOK * C * C + 2 * TOK * DV * C
+
+
+def tile_full_tmix_params_pb_t_kernel(tc, x, v_first, x_v, Wv, v0, xv_v1, v2, out):
+    nc = tc.nc
+    xf = x.flatten_outer_dims()
+    vff = v_first.flatten_outer_dims()
+    af = xv_v1.flatten_outer_dims()
+    of = out.flatten_outer_dims()
+
+    with ExitStack() as ctx:
+        ctx.enter_context(tc.manual_schedule())
+        const = ctx.enter_context(tc.tile_pool(name="const", bufs=1))
+        wpool = ctx.enter_context(tc.tile_pool(name="wpool", bufs=1))
+        xpool = ctx.enter_context(tc.tile_pool(name="xpool", bufs=3))
+        vpool = ctx.enter_context(tc.tile_pool(name="vpool", bufs=3))
+        xvpool = ctx.enter_context(tc.tile_pool(name="xvpool", bufs=3))
+        t2pool = ctx.enter_context(tc.tile_pool(name="t2pool", bufs=3))
+        gpool = ctx.enter_context(tc.tile_pool(name="gpool", bufs=2))
+        cpool = ctx.enter_context(tc.tile_pool(name="cpool", bufs=4))
+        spool = ctx.enter_context(tc.tile_pool(name="spool", bufs=3))
+        dpool = ctx.enter_context(tc.tile_pool(name="dpool", bufs=5))
+        apool = ctx.enter_context(tc.tile_pool(name="apool", bufs=2))
+        psA = ctx.enter_context(tc.psum_pool(name="psA", bufs=2))
+        psP = ctx.enter_context(tc.psum_pool(name="psP", bufs=4))
+        psZ = ctx.enter_context(tc.psum_pool(name="psZ", bufs=2))
+
+        xs_tiles = {}
+        vf_tiles = {}
+        xt_tiles = {}
+        xvp_tiles = {}
+        t2_tiles = {}
+        grp_tiles = {}
+        xc_tiles = {}
+        xsc_tiles = {}
+        pp_tiles = {}
+        zz_tiles = {}
+        gs_tiles = {}
+        d_tiles = {}
+        aT_tiles = {}
+
+        def load_x(ck, pieces):
+            xs = xpool.tile([P, 4, C], BF16, name="xs")
+            src = xf[CHUNK * ck : CHUNK * (ck + 1), :].rearrange("(t p) c -> p t c", p=P)
+            w = C // pieces
+            for i in range(pieces):
+                nc.sync.dma_start(out=xs[:, :, w * i : w * (i + 1)], in_=src[:, :, w * i : w * (i + 1)])
+            xs_tiles[ck] = xs
+
+        def load_vf(ck):
+            vt = vpool.tile([P, 4, C], BF16, name="vt")
+            nc.sync.dma_start(
+                out=vt[:],
+                in_=vff[CHUNK * ck : CHUNK * (ck + 1), :].rearrange("(t p) c -> p t c", p=P),
+            )
+            vf_tiles[ck] = vt
+
+        w_bf = const.tile([P, 2, 4], BF16, name="w_bf")
+        nc.sync.dma_start(out=w_bf[:], in_=x_v.rearrange("(g p j) -> p g j", g=2, j=4))
+        load_x(0, 4)
+        wv_sb = wpool.tile([P, 8, C], BF16, name="wv_sb")
+        wv_view = Wv.rearrange("(o p) k -> p o k", p=P)
+        for q in range(4):
+            nc.sync.dma_start(out=wv_sb[:, 2 * q : 2 * q + 2, :], in_=wv_view[:, 2 * q : 2 * q + 2, :])
+        a_sb = const.tile([P, NT, DV], BF16, name="a_sb")
+        a_view = af.rearrange("(m p) d -> p m d", p=P)
+        nc.sync.dma_start(out=a_sb[:, 0:8, :], in_=a_view[:, 0:8, :])
+        v0row = const.tile([P, P], BF16, name="v0row")
+        nc.vector.memset(v0row[:], 0.0)
+        nc.sync.dma_start(out=v0row[0:8, :], in_=v0.rearrange("(o p) -> o p", p=P))
+        v0one = const.tile([P, 512], BF16, name="v0one")
+        nc.vector.memset(v0one[:], 0.0)
+        nc.sync.dma_start(out=v0one[0:1, :], in_=v0.rearrange("(o c) -> o c", c=512)[0:1, :])
+        v2_sb = const.tile([P, C], BF16, name="v2_sb")
+        nc.sync.dma_start(out=v2_sb[:], in_=v2)
+        load_x(1, 1)
+        load_vf(0)
+        nc.sync.dma_start(out=a_sb[:, 8:NT, :], in_=a_view[:, 8:NT, :])
+        load_x(2, 1)
+
+        ident_f = const.tile([P, P], F32, name="ident_f")
+        make_identity(nc, ident_f[:])
+        ident_b = const.tile([P, P], BF16, name="ident_b")
+        make_identity(nc, ident_b[:])
+        ones_b = const.tile([P, P], BF16, name="ones_b")
+        nc.vector.memset(ones_b[:], 1.0)
+        zero4 = const.tile([P, 4], F32, name="zero4")
+        nc.vector.memset(zero4[:], 0.0)
+
+        w_col = const.tile([P, 8], F32, name="w_col")
+        nc.vector.tensor_copy(out=w_col[:], in_=w_bf[:].rearrange("p g j -> p (g j)"))
+        omw = const.tile([P, 8], F32, name="omw")
+        nc.vector.tensor_scalar(
+            out=omw[:], in0=w_col[:], scalar1=-1.0, scalar2=1.0, op0=ALU.mult, op1=ALU.add
+        )
+        v0T = const.tile([P, 4, P], F32, name="v0T")
+
+        def prep_v0():
+            v0ps = psZ.tile([P, P], BF16, name="v0ps", tag="zz")
+            nc.tensor.transpose(v0ps[:], v0row[:], ident_b[:])
+            nc.vector.tensor_copy(out=v0T[:], in_=v0ps[:, 4:8].unsqueeze(2).to_broadcast([P, 4, P]))
+
+        def prep_aT(ck):
+            aps = psZ.tile([P, CHUNK], BF16, name="aps", tag="zz")
+            for m in range(4):
+                nc.tensor.transpose(aps[:, P * m : P * (m + 1)], a_sb[:, 4 * ck + m, :], ident_b[:])
+            aT = apool.tile([P, CHUNK], BF16, name="aT")
+            nc.scalar.copy(out=aT[:], in_=aps[:])
+            aT_tiles[ck] = aT
+
+        w_codes = const.tile([P, 2, C], U32, name="w_codes", align_bytes=64)
+        w_scales = const.tile([P, 2, C], U8, name="w_scales", align_bytes=64)
+        wg0 = wpool.tile([P, 4 * C], BF16, name="wg0", align_bytes=64)
+        wg1 = wpool.tile([P, 4 * C], BF16, name="wg1", align_bytes=64)
+        wgs = [wg0, wg1]
+
+        def prep_w(q):
+            for g in range(2):
+                wt = psP.tile([P, 2, 256], F32, name="wt", tag="pp")
+                for u in range(2):
+                    for oo in range(2):
+                        nc.tensor.transpose(
+                            wt[:, u, P * oo : P * (oo + 1)],
+                            wv_sb[:, 2 * q + oo, :].bitcast(F32)[:, 256 * g + u : 256 * (g + 1) : 2],
+                            ident_f[:],
+                        )
+                w_dst = wgs[g][:, 1024 * q : 1024 * (q + 1)].bitcast(F32).rearrange("p (c u) -> p c u", u=2)
+                if g == 0:
+                    nc.vector.tensor_copy(out=w_dst, in_=wt[:].rearrange("p u c -> p c u"))
+                else:
+                    nc.scalar.copy(out=w_dst, in_=wt[:].rearrange("p u c -> p c u"))
+
+        def quant_w(h):
+            if True:
+                for g in range(2):
+                    nc.vector.quantize_mx(
+                        out=w_codes[:, g, 512 * h : 512 * (h + 1)].bitcast(FP8X4),
+                        scales=w_scales[:, g, 512 * h : 512 * (h + 1)],
+                        in_=wgs[g][:, 2048 * h : 2048 * (h + 1)],
+                    )
+
+        def xtr(a):
+            ck, i = divmod(a, 4)
+            g, u = divmod(i, 2)
+            xs = xs_tiles[ck]
+            xt = psA.tile([P, CHUNK], F32, name="xt")
+            for tt in range(4):
+                nc.tensor.transpose(
+                    xt[:, P * tt : P * (tt + 1)],
+                    xs[:, tt, :].bitcast(F32)[:, 256 * g + u : 256 * (g + 1) : 2],
+                    ident_f[:],
+                )
+            xt_tiles[a] = xt
+
+        def t2ops(a):
+            ck, i = divmod(a, 4)
+            g, u = divmod(i, 2)
+            if u == 0:
+                t2 = t2pool.tile([P, 4, TW], F32, name="t2")
+                t2_tiles[(ck, g)] = t2
+                if ck % SEQ_CHUNKS == 0:
+                    nc.scalar.copy(out=t2[:, :, 0:1], in_=zero4[:].unsqueeze(2))
+                else:
+                    nc.scalar.copy(
+                        out=t2[:, :, 0:1], in_=t2_tiles[(ck - 1, g)][:, :, CHUNK : CHUNK + 1]
+                    )
+            t2 = t2_tiles[(ck, g)]
+            xb = xt_tiles[a][:].bitcast(BF16).rearrange("p (t e) -> p t e", e=2)
+            for e in range(2):
+                j = 2 * u + e
+                pl = 4 * g + j
+                nc.scalar.activation(
+                    out=t2[:, j, 1 : CHUNK + 1], in_=xb[:, :, e], func=ACT.Copy, scale=w_col[:, pl : pl + 1]
+                )
+
+        def a2ops(a):
+            ck, i = divmod(a, 4)
+            g, u = divmod(i, 2)
+            if u == 0:
+                xvp = xvpool.tile([P, 4, CHUNK], BF16, name="xvp")
+                xvp_tiles[(ck, g)] = xvp
+            xvp = xvp_tiles[(ck, g)]
+            t2 = t2_tiles[(ck, g)]
+            xb = xt_tiles[a][:].bitcast(BF16).rearrange("p (t e) -> p t e", e=2)
+            for e in range(2):
+                j = 2 * u + e
+                pl = 4 * g + j
+                nc.vector.scalar_tensor_tensor(
+                    out=xvp[:, j, :],
+                    in0=xb[:, :, e],
+                    scalar=omw[:, pl : pl + 1],
+                    in1=t2[:, j, 0:CHUNK],
+                    op0=ALU.mult,
+                    op1=ALU.add,
+                )
+
+        def rg(r):
+            ck, rr = divmod(r, 4)
+            g, hh = divmod(rr, 2)
+            if hh == 0:
+                grp = gpool.tile([P, CHUNK, 4], BF16, name="grp", align_bytes=64)
+                grp_tiles[(ck, g)] = grp
+            grp = grp_tiles[(ck, g)]
+            xvp = xvp_tiles[(ck, g)]
+            lo = HALF * hh
+            nc.scalar.copy(
+                out=grp[:, lo : lo + HALF, :].rearrange("p (c i) j -> p c j i", i=4),
+                in_=xvp[:, :, lo : lo + HALF].rearrange("p j (c i) -> p c j i", i=4),
+            )
+
+        def quanth(r):
+            ck, rr = divmod(r, 4)
+            g, hh = divmod(rr, 2)
+            if hh == 0:
+                xc = cpool.tile([P, CHUNK], U32, name="xc", align_bytes=64)
+                xsc = cpool.tile([P, CHUNK], U8, name="xsc", align_bytes=64)
+                xc_tiles[(ck, g)] = xc
+                xsc_tiles[(ck, g)] = xsc
+            lo = HALF * hh
+            nc.vector.quantize_mx(
+                out=xc_tiles[(ck, g)][:, lo : lo + HALF].bitcast(FP8X4),
+                scales=xsc_tiles[(ck, g)][:, lo : lo + HALF],
+                in_=grp_tiles[(ck, g)][:, lo : lo + HALF, :].rearrange("p t j -> p (t j)"),
+            )
+
+        def mx(n):
+            ck, tt = divmod(n, 4)
+            ts = slice(P * tt, P * (tt + 1))
+            for h in range(2):
+                cs = slice(512 * h, 512 * (h + 1))
+                pp = psP.tile([P, 512], F32, name="pp")
+                pp_tiles[(n, h)] = pp
+                for g in range(2):
+                    nc.tensor.matmul_mx(
+                        out=pp[:],
+                        lhsT=xc_tiles[(ck, g)][:, ts].bitcast(FP8X4),
+                        lhsT_scale=xsc_tiles[(ck, g)][:, ts],
+                        rhs=w_codes[:, g, cs].bitcast(FP8X4),
+                        rhs_scale=w_scales[:, g, cs],
+                        start=(g == 0),
+                        stop=(g == 1),
+                    )
+
+        def zgrp(n):
+            ck, tt = divmod(n, 4)
+            for h in (1, 0):
+                cs = slice(512 * h, 512 * (h + 1))
+                zz = psZ.tile([P, 512], F32, name="zz")
+                zz_tiles[(n, h)] = zz
+                if h == 0:
+                    nc.tensor.matmul(out=zz[:], lhsT=ones_b[:], rhs=v0one[:], start=True, stop=False)
+                else:
+                    for i in range(4):
+                        nc.tensor.matmul(
+                            out=zz[:, P * i : P * (i + 1)],
+                            lhsT=v0T[:, i, :],
+                            rhs=ident_f[:],
+                            is_transpose=True,
+                            start=(i == 0),
+                            stop=False,
+                        )
+                nc.tensor.matmul(
+                    out=zz[:], lhsT=aT_tiles[ck][:, P * tt : P * (tt + 1)], rhs=v2_sb[:, cs], start=False, stop=True
+                )
+
+        def sig(n):
+            gs = spool.tile([P, C], F32, name="gs")
+            gs_tiles[n] = gs
+            for h in (1, 0):
+                nc.scalar.activation(
+                    out=gs[:, 512 * h : 512 * (h + 1)], in_=zz_tiles[(n, h)][:], func=ACT.Sigmoid
+                )
+
+        def v1(n):
+            ck, tt = divmod(n, 4)
+            d = dpool.tile([P, C], F32, name="d")
+            d_tiles[n] = d
+            for h in range(2):
+                cs = slice(512 * h, 512 * (h + 1))
+                nc.vector.tensor_tensor(
+                    out=d[:, cs], in0=vf_tiles[ck][:, tt, cs], in1=pp_tiles[(n, h)][:], op=ALU.subtract
+                )
+
+        def v2op(n):
+            d = d_tiles[n]
+            nc.gpsimd.tensor_tensor(out=d[:], in0=d[:], in1=gs_tiles[n][:], op=ALU.mult)
+
+        def fin(n):
+            d = d_tiles[n]
+            for h in range(2):
+                cs = slice(512 * h, 512 * (h + 1))
+                nc.vector.tensor_tensor(out=d[:, cs], in0=d[:, cs], in1=pp_tiles[(n, h)][:], op=ALU.add)
+                nc.sync.dma_start(out=of[P * n : P * (n + 1), cs], in_=d[:, cs])
+
+        for n in range(-7, NT + 1):
+            if 0 <= n - 1 < NT:
+                fin(n - 1)
+            if (n + 15) % 4 == 0 and 3 <= (n + 15) // 4 < NCHUNK:
+                load_x((n + 15) // 4, 1)
+            if (n + 9) % 4 == 0 and 1 <= (n + 9) // 4 < NCHUNK:
+                load_vf((n + 9) // 4)
+            if 0 <= n + 7 < NT:
+                xtr(n + 7)
+            if 0 <= n + 1 < NT:
+                sig(n + 1)
+            if n == -3:
+                prep_v0()
+            if (n + 3) % 4 == 0 and 0 <= (n + 3) // 4 < NCHUNK:
+                prep_aT((n + 3) // 4)
+            if 0 <= n + 1 < NT:
+                mx(n + 1)
+            if 0 <= n + 2 < NT:
+                zgrp(n + 2)
+            if 0 <= n + 4 < NT:
+                rg(n + 4)
+            if 0 <= n + 7 < NT:
+                t2ops(n + 7)
+            if 0 <= n + 6 < NT:
+                a2ops(n + 6)
+            if -6 <= n <= -3:
+                prep_w(n + 6)
+            if n == -4 or n == -2:
+                quant_w((n + 4) // 2)
+            if 0 <= n + 1 < NT:
+                v1(n + 1)
+            if 0 <= n + 4 < NT:
+                quanth(n + 4)
+            if 0 <= n + 1 < NT:
+                v2op(n + 1)

@@ -21,6 +21,7 @@ NT = TOK // P
 SEQ_CHUNKS = 1024 // CHUNK
 TW = CHUNK + 4
 HALF = CHUNK // 2
+HEAD_RG = 4
 
 FLOPS = 2 * TOK * C * C + 2 * TOK * DV * C
 
@@ -227,10 +228,12 @@ def tile_full_tmix_params_pb_t_kernel(tc, x, v_first, x_v, Wv, v0, xv_v1, v2, ou
             grp = grp_tiles[(ck, g)]
             xvp = xvp_tiles[(ck, g)]
             lo = HALF * hh
-            nc.scalar.copy(
-                out=grp[:, lo : lo + HALF, :].rearrange("p (c i) j -> p c j i", i=4),
-                in_=xvp[:, :, lo : lo + HALF].rearrange("p j (c i) -> p c j i", i=4),
-            )
+            dst = grp[:, lo : lo + HALF, :].rearrange("p (c i) j -> p c j i", i=4)
+            src = xvp[:, :, lo : lo + HALF].rearrange("p j (c i) -> p c j i", i=4)
+            if r < HEAD_RG:
+                nc.gpsimd.tensor_scalar(out=dst, in0=src, scalar1=1.0, scalar2=0.0, op0=ALU.mult, op1=ALU.add)
+            else:
+                nc.scalar.copy(out=dst, in_=src)
 
         def quanth(r):
             ck, rr = divmod(r, 4)

@@ -123,7 +123,7 @@ def tile_full_tmix_params_pb_t_kernel(tc, x, v_first, x_v, Wv, v0, xv_v1, v2, ou
         def prep_v0():
             v0ps = psZ.tile([P, P], BF16, name="v0ps", tag="zz")
             nc.tensor.transpose(v0ps[:], v0row[:], ident_b[:])
-            nc.vector.tensor_copy(out=v0T[:], in_=v0ps[:, 4:8].unsqueeze(2).to_broadcast([P, 4, P]))
+            nc.scalar.copy(out=v0T[:], in_=v0ps[:, 4:8].unsqueeze(2).to_broadcast([P, 4, P]))
 
         def prep_aT(ck):
             aps = psZ.tile([P, CHUNK], BF16, name="aps", tag="zz")
@@ -150,10 +150,7 @@ def tile_full_tmix_params_pb_t_kernel(tc, x, v_first, x_v, Wv, v0, xv_v1, v2, ou
                             ident_f[:],
                         )
                 w_dst = wgs[g][:, 1024 * q : 1024 * (q + 1)].bitcast(F32).rearrange("p (c u) -> p c u", u=2)
-                if g == 0:
-                    nc.vector.tensor_copy(out=w_dst, in_=wt[:].rearrange("p u c -> p c u"))
-                else:
-                    nc.scalar.copy(out=w_dst, in_=wt[:].rearrange("p u c -> p c u"))
+                nc.scalar.copy(out=w_dst, in_=wt[:].rearrange("p u c -> p c u"))
 
         def quant_w(h):
             if True:
@@ -310,7 +307,12 @@ def tile_full_tmix_params_pb_t_kernel(tc, x, v_first, x_v, Wv, v0, xv_v1, v2, ou
 
         def v2op(n):
             d = d_tiles[n]
-            nc.gpsimd.tensor_tensor(out=d[:], in0=d[:], in1=gs_tiles[n][:], op=ALU.mult)
+            if n < NT - 1:
+                nc.gpsimd.tensor_tensor(out=d[:], in0=d[:], in1=gs_tiles[n][:], op=ALU.mult)
+            else:
+                for h in range(2):
+                    cs = slice(512 * h, 512 * (h + 1))
+                    nc.gpsimd.tensor_tensor(out=d[:, cs], in0=d[:, cs], in1=gs_tiles[n][:, cs], op=ALU.mult)
 
         def fin(n):
             d = d_tiles[n]

@@ -22,6 +22,8 @@ SEQ_CHUNKS = 1024 // CHUNK
 TW = CHUNK + 4
 HALF = CHUNK // 2
 HEAD_RG = 4
+GP = 4
+GW = 512 // GP
 
 FLOPS = 2 * TOK * C * C + 2 * TOK * DV * C
 
@@ -44,7 +46,7 @@ def tile_full_tmix_params_pb_t_kernel(tc, x, v_first, x_v, Wv, v0, xv_v1, v2, ou
         gpool = ctx.enter_context(tc.tile_pool(name="gpool", bufs=2))
         cpool = ctx.enter_context(tc.tile_pool(name="cpool", bufs=4))
         spool = ctx.enter_context(tc.tile_pool(name="spool", bufs=3))
-        dpool = ctx.enter_context(tc.tile_pool(name="dpool", bufs=5))
+        dpool = ctx.enter_context(tc.tile_pool(name="dpool", bufs=8))
         apool = ctx.enter_context(tc.tile_pool(name="apool", bufs=2))
         psA = ctx.enter_context(tc.psum_pool(name="psA", bufs=2))
         psP = ctx.enter_context(tc.psum_pool(name="psP", bufs=4))
@@ -287,12 +289,18 @@ def tile_full_tmix_params_pb_t_kernel(tc, x, v_first, x_v, Wv, v0, xv_v1, v2, ou
                     out=zz[:], lhsT=aT_tiles[ck][:, P * tt : P * (tt + 1)], rhs=v2_sb[:, cs], start=False, stop=True
                 )
 
+        def gp_ends(n):
+            return n % 4 == 0 and n < NT - 7
+
         def sig(n):
             gs = spool.tile([P, C], F32, name="gs")
             gs_tiles[n] = gs
             for h in (1, 0):
                 nc.scalar.activation(
-                    out=gs[:, 512 * h : 512 * (h + 1)], in_=zz_tiles[(n, h)][:], func=ACT.Sigmoid
+                    out=gs[:, 512 * h : 512 * (h + 1)],
+                    in_=zz_tiles[(n, h)][:],
+                    func=ACT.Sigmoid,
+                    scale=(-1.0 if (h == 1 and gp_ends(n)) else 1.0),
                 )
 
         def v1(n):
@@ -314,9 +322,20 @@ def tile_full_tmix_params_pb_t_kernel(tc, x, v_first, x_v, Wv, v0, xv_v1, v2, ou
                     cs = slice(512 * h, 512 * (h + 1))
                     nc.gpsimd.tensor_tensor(out=d[:, cs], in0=d[:, cs], in1=gs_tiles[n][:, cs], op=ALU.mult)
 
+        def gp_piece(n, k):
+            ck, tt = divmod(n, 4)
+            d = d_tiles[n]
+            cs = slice(512 + GW * k, 512 + GW * (k + 1))
+            nc.gpsimd.tensor_tensor(out=d[:, cs], in0=vf_tiles[ck][:, tt, cs], in1=d[:, cs], op=ALU.subtract)
+
+        def gp_store(n):
+            nc.sync.dma_start(out=of[P * n : P * (n + 1), 512:1024], in_=d_tiles[n][:, 512:1024])
+
         def fin(n):
             d = d_tiles[n]
             for h in range(2):
+                if h == 1 and gp_ends(n):
+                    continue
                 cs = slice(512 * h, 512 * (h + 1))
                 nc.vector.tensor_tensor(out=d[:, cs], in0=d[:, cs], in1=pp_tiles[(n, h)][:], op=ALU.add)
                 nc.sync.dma_start(out=of[P * n : P * (n + 1), cs], in_=d[:, cs])
@@ -356,3 +375,8 @@ def tile_full_tmix_params_pb_t_kernel(tc, x, v_first, x_v, Wv, v0, xv_v1, v2, ou
                 quanth(n + 4)
             if 0 <= n + 1 < NT:
                 v2op(n + 1)
+            for k in range(GP):
+                if 0 <= n + 1 - k < NT and gp_ends(n + 1 - k):
+                    gp_piece(n + 1 - k, k)
+            if 0 <= n + 1 - GP < NT and gp_ends(n + 1 - GP):
+                gp_store(n + 1 - GP)

@@ -83,8 +83,15 @@ def tile_full_tmix_params_pb_t_kernel(tc, x, v_first, x_v, Wv, v0, xv_v1, v2, ou
             vf_tiles[ck] = vt
 
         w_bf = const.tile([P, 2, 4], BF16, name="w_bf")
-        nc.sync.dma_start(out=w_bf[:], in_=x_v.rearrange("(g p j) -> p g j", g=2, j=4))
-        load_x(0, 4)
+        nc.scalar.dma_start(out=w_bf[:], in_=x_v.rearrange("(g p j) -> p g j", g=2, j=4))
+        xs0 = xpool.tile([P, 4, C], BF16, name="xs")
+        xs_tiles[0] = xs0
+        src0 = xf[0:CHUNK, :].rearrange("(t p) c -> p t c", p=P)
+        for hh in range(2):
+            nc.sync.dma_start(
+                out=xs0[:, 2 * hh : 2 * hh + 2, 0:512], in_=src0[:, 2 * hh : 2 * hh + 2, 0:512]
+            )
+        nc.sync.dma_start(out=xs0[:, :, 512:C], in_=src0[:, :, 512:C])
         wv_sb = wpool.tile([P, 8, C], BF16, name="wv_sb")
         wv_view = Wv.rearrange("(o p) k -> p o k", p=P)
         for q in range(4):
@@ -100,7 +107,7 @@ def tile_full_tmix_params_pb_t_kernel(tc, x, v_first, x_v, Wv, v0, xv_v1, v2, ou
         nc.sync.dma_start(out=v0one[0:1, :], in_=v0.rearrange("(o c) -> o c", c=512)[0:1, :])
         v2_sb = const.tile([P, C], BF16, name="v2_sb")
         nc.sync.dma_start(out=v2_sb[:], in_=v2)
-        load_x(1, 1)
+        load_x(1, 4)
         load_vf(0)
         nc.sync.dma_start(out=a_sb[:, 8:NT, :], in_=a_view[:, 8:NT, :])
         load_x(2, 1)
@@ -113,6 +120,8 @@ def tile_full_tmix_params_pb_t_kernel(tc, x, v_first, x_v, Wv, v0, xv_v1, v2, ou
         nc.vector.memset(ones_b[:], 1.0)
         zero4 = const.tile([P, 4], F32, name="zero4")
         nc.vector.memset(zero4[:], 0.0)
+        table_first = const.tile([P, 1], F32, name="table_first")
+        nc.scalar.activation(out=table_first[:], in_=zero4[:, 0:1], func=ACT.Sigmoid)
 
         w_col = const.tile([P, 8], F32, name="w_col")
         nc.vector.tensor_copy(out=w_col[:], in_=w_bf[:].rearrange("p g j -> p (g j)"))
@@ -162,6 +171,54 @@ def tile_full_tmix_params_pb_t_kernel(tc, x, v_first, x_v, Wv, v0, xv_v1, v2, ou
                         scales=w_scales[:, g, 512 * h : 512 * (h + 1)],
                         in_=wgs[g][:, 2048 * h : 2048 * (h + 1)],
                     )
+
+        half_xt = {}
+
+        def half_xtr(hh, u):
+            if hh == 0:
+                xt = psZ.tile([P, HALF], F32, name="xt", tag="zz")
+            else:
+                xt = psA.tile([P, HALF], F32, name="xt", tag="xt")
+            for tt in range(2):
+                nc.tensor.transpose(
+                    xt[:, P * tt : P * (tt + 1)],
+                    xs0[:, 2 * hh + tt, :].bitcast(F32)[:, u:256:2],
+                    ident_f[:],
+                )
+            half_xt[(hh, u)] = xt
+
+        def half_t2(hh, u):
+            if hh == 0 and u == 0:
+                t2 = t2pool.tile([P, 4, TW], F32, name="t2")
+                t2_tiles[(0, 0)] = t2
+                nc.scalar.copy(out=t2[:, :, 0:1], in_=zero4[:].unsqueeze(2))
+            t2 = t2_tiles[(0, 0)]
+            xb = half_xt[(hh, u)][:].bitcast(BF16).rearrange("p (t e) -> p t e", e=2)
+            for e in range(2):
+                j = 2 * u + e
+                nc.scalar.activation(
+                    out=t2[:, j, HALF * hh + 1 : HALF * (hh + 1) + 1],
+                    in_=xb[:, :, e],
+                    func=ACT.Copy,
+                    scale=w_col[:, j : j + 1],
+                )
+
+        def half_a2(hh, u):
+            if hh == 0 and u == 0:
+                xvp = xvpool.tile([P, 4, CHUNK], BF16, name="xvp")
+                xvp_tiles[(0, 0)] = xvp
+            ts = slice(HALF * hh, HALF * (hh + 1))
+            xb = half_xt[(hh, u)][:].bitcast(BF16).rearrange("p (t e) -> p t e", e=2)
+            for e in range(2):
+                j = 2 * u + e
+                nc.vector.scalar_tensor_tensor(
+                    out=xvp_tiles[(0, 0)][:, j, ts],
+                    in0=xb[:, :, e],
+                    scalar=omw[:, j : j + 1],
+                    in1=t2_tiles[(0, 0)][:, j, ts],
+                    op0=ALU.mult,
+                    op1=ALU.add,
+                )
 
         def xtr(a):
             ck, i = divmod(a, 4)
@@ -254,7 +311,10 @@ def tile_full_tmix_params_pb_t_kernel(tc, x, v_first, x_v, Wv, v0, xv_v1, v2, ou
             ts = slice(P * tt, P * (tt + 1))
             for h in range(2):
                 cs = slice(512 * h, 512 * (h + 1))
-                pp = psP.tile([P, 512], F32, name="pp")
+                if n >= NT - 5 and n % 2 == 1:
+                    pp = psA.tile([P, 512], F32, name="pp", tag="xt")
+                else:
+                    pp = psP.tile([P, 512], F32, name="pp")
                 pp_tiles[(n, h)] = pp
                 for g in range(2):
                     nc.tensor.matmul_mx(
@@ -290,7 +350,7 @@ def tile_full_tmix_params_pb_t_kernel(tc, x, v_first, x_v, Wv, v0, xv_v1, v2, ou
                 )
 
         def gp_ends(n):
-            return n % 4 == 0 and n < NT - 7
+            return n % 4 == 0 and n < NT - 11
 
         def sig(n):
             gs = spool.tile([P, C], F32, name="gs")
@@ -318,9 +378,15 @@ def tile_full_tmix_params_pb_t_kernel(tc, x, v_first, x_v, Wv, v0, xv_v1, v2, ou
             if n < NT - 1:
                 nc.gpsimd.tensor_tensor(out=d[:], in0=d[:], in1=gs_tiles[n][:], op=ALU.mult)
             else:
-                for h in range(2):
-                    cs = slice(512 * h, 512 * (h + 1))
-                    nc.gpsimd.tensor_tensor(out=d[:, cs], in0=d[:, cs], in1=gs_tiles[n][:, cs], op=ALU.mult)
+                nc.gpsimd.tensor_tensor(
+                    out=d[:, 0:512], in0=d[:, 0:512], in1=gs_tiles[n][:, 0:512], op=ALU.mult
+                )
+
+        def last_v2op():
+            d = d_tiles[NT - 1]
+            nc.vector.tensor_tensor(
+                out=d[:, 512:C], in0=d[:, 512:C], in1=gs_tiles[NT - 1][:, 512:C], op=ALU.mult
+            )
 
         def gp_piece(n, k):
             ck, tt = divmod(n, 4)
@@ -340,9 +406,24 @@ def tile_full_tmix_params_pb_t_kernel(tc, x, v_first, x_v, Wv, v0, xv_v1, v2, ou
                 nc.vector.tensor_tensor(out=d[:, cs], in0=d[:, cs], in1=pp_tiles[(n, h)][:], op=ALU.add)
                 nc.sync.dma_start(out=of[P * n : P * (n + 1), cs], in_=d[:, cs])
 
-        for n in range(-7, NT + 1):
+        half_xtr(0, 0)
+        half_t2(0, 0)
+        half_xtr(0, 1)
+        half_t2(0, 1)
+        half_a2(0, 0)
+        half_xtr(1, 0)
+        half_t2(1, 0)
+        half_a2(0, 1)
+        half_xtr(1, 1)
+        half_t2(1, 1)
+        half_a2(1, 0)
+        prep_w(0)
+        half_a2(1, 1)
+        for n in range(-5, NT + 1):
             if 0 <= n - 1 < NT:
                 fin(n - 1)
+            if n == NT - 1:
+                last_v2op()
             if (n + 15) % 4 == 0 and 3 <= (n + 15) // 4 < NCHUNK:
                 load_x((n + 15) // 4, 1)
             if (n + 9) % 4 == 0 and 1 <= (n + 9) // 4 < NCHUNK:
@@ -363,9 +444,9 @@ def tile_full_tmix_params_pb_t_kernel(tc, x, v_first, x_v, Wv, v0, xv_v1, v2, ou
                 rg(n + 4)
             if 0 <= n + 7 < NT:
                 t2ops(n + 7)
-            if 0 <= n + 6 < NT:
+            if 2 <= n + 6 < NT:
                 a2ops(n + 6)
-            if -6 <= n <= -3:
+            if -5 <= n <= -3:
                 prep_w(n + 6)
             if n == -4 or n == -2:
                 quant_w((n + 4) // 2)

@@ -150,27 +150,29 @@ def tile_full_tmix_params_pb_t_kernel(tc, x, v_first, x_v, Wv, v0, xv_v1, v2, ou
         wg1 = wpool.tile([P, 4 * C], BF16, name="wg1", align_bytes=64)
         wgs = [wg0, wg1]
 
-        def prep_w(q):
-            for g in range(2):
-                wt = psP.tile([P, 2, 256], F32, name="wt", tag="pp")
-                for u in range(2):
-                    for oo in range(2):
-                        nc.tensor.transpose(
-                            wt[:, u, P * oo : P * (oo + 1)],
-                            wv_sb[:, 2 * q + oo, :].bitcast(F32)[:, 256 * g + u : 256 * (g + 1) : 2],
-                            ident_f[:],
-                        )
-                w_dst = wgs[g][:, 1024 * q : 1024 * (q + 1)].bitcast(F32).rearrange("p (c u) -> p c u", u=2)
-                nc.scalar.copy(out=w_dst, in_=wt[:].rearrange("p u c -> p c u"))
+        def prep_w(q, g):
+            wt = psP.tile([P, 2, 256], F32, name="wt", tag="pp")
+            for u in range(2):
+                for oo in range(2):
+                    nc.tensor.transpose(
+                        wt[:, u, P * oo : P * (oo + 1)],
+                        wv_sb[:, 2 * q + oo, :].bitcast(F32)[:, 256 * g + u : 256 * (g + 1) : 2],
+                        ident_f[:],
+                    )
+            w_dst = wgs[g][:, 1024 * q : 1024 * (q + 1)].bitcast(F32).rearrange("p (c u) -> p c u", u=2)
+            w_src = wt[:].rearrange("p u c -> p c u")
+            if q == 0:
+                nc.vector.tensor_copy(out=w_dst, in_=w_src)
+            else:
+                nc.scalar.copy(out=w_dst, in_=w_src)
 
         def quant_w(h):
-            if True:
-                for g in range(2):
-                    nc.vector.quantize_mx(
-                        out=w_codes[:, g, 512 * h : 512 * (h + 1)].bitcast(FP8X4),
-                        scales=w_scales[:, g, 512 * h : 512 * (h + 1)],
-                        in_=wgs[g][:, 2048 * h : 2048 * (h + 1)],
-                    )
+            for g in range(2):
+                nc.vector.quantize_mx(
+                    out=w_codes[:, g, 512 * h : 512 * (h + 1)].bitcast(FP8X4),
+                    scales=w_scales[:, g, 512 * h : 512 * (h + 1)],
+                    in_=wgs[g][:, 2048 * h : 2048 * (h + 1)],
+                )
 
         half_xt = {}
 
@@ -311,7 +313,7 @@ def tile_full_tmix_params_pb_t_kernel(tc, x, v_first, x_v, Wv, v0, xv_v1, v2, ou
             ts = slice(P * tt, P * (tt + 1))
             for h in range(2):
                 cs = slice(512 * h, 512 * (h + 1))
-                if n >= NT - 5 and n % 2 == 1:
+                if n >= NT - 5 and n % 3 == 0:
                     pp = psA.tile([P, 512], F32, name="pp", tag="xt")
                 else:
                     pp = psP.tile([P, 512], F32, name="pp")
@@ -417,44 +419,71 @@ def tile_full_tmix_params_pb_t_kernel(tc, x, v_first, x_v, Wv, v0, xv_v1, v2, ou
         half_xtr(1, 1)
         half_t2(1, 1)
         half_a2(1, 0)
-        prep_w(0)
+        rg(0)
+        prep_w(0, 0)
+        xtr(2)
+        t2ops(2)
         half_a2(1, 1)
-        for n in range(-5, NT + 1):
+        prep_w(0, 1)
+        a2ops(2)
+        prep_w(1, 0)
+        prep_w(1, 1)
+        xtr(3)
+        t2ops(3)
+        prep_v0()
+        prep_w(2, 0)
+        prep_w(2, 1)
+        quant_w(0)
+        rg(1)
+        quanth(0)
+        a2ops(3)
+        prep_w(3, 1)
+        xtr(4)
+        t2ops(4)
+        prep_aT(0)
+        prep_w(3, 0)
+        rg(2)
+        rg(3)
+        quanth(1)
+        a2ops(4)
+        quanth(2)
+        xtr(5)
+        t2ops(5)
+        quant_w(1)
+        quanth(3)
+        zgrp(0)
+        load_vf(1)
+        load_x(3, 1)
+        for n in range(-1, NT + 1):
             if 0 <= n - 1 < NT:
                 fin(n - 1)
             if n == NT - 1:
                 last_v2op()
-            if (n + 15) % 4 == 0 and 3 <= (n + 15) // 4 < NCHUNK:
+            if (n + 15) % 4 == 0 and 4 <= (n + 15) // 4 < NCHUNK:
                 load_x((n + 15) // 4, 1)
-            if (n + 9) % 4 == 0 and 1 <= (n + 9) // 4 < NCHUNK:
+            if (n + 9) % 4 == 0 and 2 <= (n + 9) // 4 < NCHUNK:
                 load_vf((n + 9) // 4)
-            if 0 <= n + 7 < NT:
+            if n + 7 < NT:
                 xtr(n + 7)
-            if 0 <= n + 1 < NT:
+            if n + 1 < NT:
                 sig(n + 1)
-            if n == -3:
-                prep_v0()
-            if (n + 3) % 4 == 0 and 0 <= (n + 3) // 4 < NCHUNK:
+            if (n + 3) % 4 == 0 and 1 <= (n + 3) // 4 < NCHUNK:
                 prep_aT((n + 3) // 4)
-            if 0 <= n + 1 < NT:
+            if n + 1 < NT:
                 mx(n + 1)
-            if 0 <= n + 2 < NT:
+            if n + 2 < NT:
                 zgrp(n + 2)
-            if 0 <= n + 4 < NT:
+            if 4 <= n + 4 < NT:
                 rg(n + 4)
-            if 0 <= n + 7 < NT:
+            if n + 7 < NT:
                 t2ops(n + 7)
-            if 2 <= n + 6 < NT:
+            if n + 6 < NT:
                 a2ops(n + 6)
-            if -5 <= n <= -3:
-                prep_w(n + 6)
-            if n == -4 or n == -2:
-                quant_w((n + 4) // 2)
-            if 0 <= n + 1 < NT:
+            if n + 1 < NT:
                 v1(n + 1)
-            if 0 <= n + 4 < NT:
+            if 4 <= n + 4 < NT:
                 quanth(n + 4)
-            if 0 <= n + 1 < NT:
+            if n + 1 < NT:
                 v2op(n + 1)
             for k in range(GP):
                 if 0 <= n + 1 - k < NT and gp_ends(n + 1 - k):

@@ -22,8 +22,8 @@ SEQ_CHUNKS = 1024 // CHUNK
 TW = CHUNK + 4
 HALF = CHUNK // 2
 HEAD_RG = 4
-GP = 4
-GW = 512 // GP
+GW = 192
+GC = 1024 - GW
 
 FLOPS = 2 * TOK * C * C + 2 * TOK * DV * C
 
@@ -352,17 +352,21 @@ def tile_full_tmix_params_pb_t_kernel(tc, x, v_first, x_v, Wv, v0, xv_v1, v2, ou
                 )
 
         def gp_ends(n):
-            return n % 4 == 0 and n < NT - 11
+            return n < NT - 6
 
         def sig(n):
             gs = spool.tile([P, C], F32, name="gs")
             gs_tiles[n] = gs
-            for h in (1, 0):
+            if gp_ends(n):
+                parts = [(1, 512, GC, 1.0), (1, GC, C, -1.0), (0, 0, 512, 1.0)]
+            else:
+                parts = [(1, 512, C, 1.0), (0, 0, 512, 1.0)]
+            for h, lo, hi, sign in parts:
                 nc.scalar.activation(
-                    out=gs[:, 512 * h : 512 * (h + 1)],
-                    in_=zz_tiles[(n, h)][:],
+                    out=gs[:, lo:hi],
+                    in_=zz_tiles[(n, h)][:, lo - 512 * h : hi - 512 * h],
                     func=ACT.Sigmoid,
-                    scale=(-1.0 if (h == 1 and gp_ends(n)) else 1.0),
+                    scale=sign,
                 )
 
         def v1(n):
@@ -390,22 +394,20 @@ def tile_full_tmix_params_pb_t_kernel(tc, x, v_first, x_v, Wv, v0, xv_v1, v2, ou
                 out=d[:, 512:C], in0=d[:, 512:C], in1=gs_tiles[NT - 1][:, 512:C], op=ALU.mult
             )
 
-        def gp_piece(n, k):
+        def gp_piece(n):
             ck, tt = divmod(n, 4)
             d = d_tiles[n]
-            cs = slice(512 + GW * k, 512 + GW * (k + 1))
-            nc.gpsimd.tensor_tensor(out=d[:, cs], in0=vf_tiles[ck][:, tt, cs], in1=d[:, cs], op=ALU.subtract)
-
-        def gp_store(n):
-            nc.sync.dma_start(out=of[P * n : P * (n + 1), 512:1024], in_=d_tiles[n][:, 512:1024])
+            nc.gpsimd.tensor_tensor(out=d[:, GC:C], in0=vf_tiles[ck][:, tt, GC:C], in1=d[:, GC:C], op=ALU.subtract)
 
         def fin(n):
             d = d_tiles[n]
             for h in range(2):
-                if h == 1 and gp_ends(n):
-                    continue
-                cs = slice(512 * h, 512 * (h + 1))
-                nc.vector.tensor_tensor(out=d[:, cs], in0=d[:, cs], in1=pp_tiles[(n, h)][:], op=ALU.add)
+                lo = 512 * h
+                hi = GC if (h == 1 and gp_ends(n)) else lo + 512
+                nc.vector.tensor_tensor(
+                    out=d[:, lo:hi], in0=d[:, lo:hi], in1=pp_tiles[(n, h)][:, 0 : hi - lo], op=ALU.add
+                )
+                cs = slice(lo, lo + 512)
                 nc.sync.dma_start(out=of[P * n : P * (n + 1), cs], in_=d[:, cs])
 
         half_xtr(0, 0)
@@ -485,8 +487,5 @@ def tile_full_tmix_params_pb_t_kernel(tc, x, v_first, x_v, Wv, v0, xv_v1, v2, ou
                 quanth(n + 4)
             if n + 1 < NT:
                 v2op(n + 1)
-            for k in range(GP):
-                if 0 <= n + 1 - k < NT and gp_ends(n + 1 - k):
-                    gp_piece(n + 1 - k, k)
-            if 0 <= n + 1 - GP < NT and gp_ends(n + 1 - GP):
-                gp_store(n + 1 - GP)
+            if n + 1 < NT and gp_ends(n + 1):
+                gp_piece(n + 1)

@@ -22,7 +22,7 @@ SEQ_CHUNKS = 1024 // CHUNK
 TW = CHUNK + 4
 HALF = CHUNK // 2
 HEAD_RG = 4
-GW = 192
+GW = 224
 GC = 1024 - GW
 
 FLOPS = 2 * TOK * C * C + 2 * TOK * DV * C
@@ -87,10 +87,8 @@ def tile_full_tmix_params_pb_t_kernel(tc, x, v_first, x_v, Wv, v0, xv_v1, v2, ou
         xs0 = xpool.tile([P, 4, C], BF16, name="xs")
         xs_tiles[0] = xs0
         src0 = xf[0:CHUNK, :].rearrange("(t p) c -> p t c", p=P)
-        for hh in range(2):
-            nc.sync.dma_start(
-                out=xs0[:, 2 * hh : 2 * hh + 2, 0:512], in_=src0[:, 2 * hh : 2 * hh + 2, 0:512]
-            )
+        for lo, hi in ((0, 1), (1, 2), (2, 4)):
+            nc.sync.dma_start(out=xs0[:, lo:hi, 0:512], in_=src0[:, lo:hi, 0:512])
         nc.sync.dma_start(out=xs0[:, :, 512:C], in_=src0[:, :, 512:C])
         wv_sb = wpool.tile([P, 8, C], BF16, name="wv_sb")
         wv_view = Wv.rearrange("(o p) k -> p o k", p=P)
@@ -98,6 +96,7 @@ def tile_full_tmix_params_pb_t_kernel(tc, x, v_first, x_v, Wv, v0, xv_v1, v2, ou
             nc.sync.dma_start(out=wv_sb[:, 2 * q : 2 * q + 2, :], in_=wv_view[:, 2 * q : 2 * q + 2, :])
         a_sb = const.tile([P, NT, DV], BF16, name="a_sb")
         a_view = af.rearrange("(m p) d -> p m d", p=P)
+        load_x(1, 4)
         nc.sync.dma_start(out=a_sb[:, 0:8, :], in_=a_view[:, 0:8, :])
         v0row = const.tile([P, P], BF16, name="v0row")
         nc.vector.memset(v0row[:], 0.0)
@@ -107,7 +106,6 @@ def tile_full_tmix_params_pb_t_kernel(tc, x, v_first, x_v, Wv, v0, xv_v1, v2, ou
         nc.sync.dma_start(out=v0one[0:1, :], in_=v0.rearrange("(o c) -> o c", c=512)[0:1, :])
         v2_sb = const.tile([P, C], BF16, name="v2_sb")
         nc.sync.dma_start(out=v2_sb[:], in_=v2)
-        load_x(1, 4)
         load_vf(0)
         nc.sync.dma_start(out=a_sb[:, 8:NT, :], in_=a_view[:, 8:NT, :])
         load_x(2, 1)
@@ -160,11 +158,7 @@ def tile_full_tmix_params_pb_t_kernel(tc, x, v_first, x_v, Wv, v0, xv_v1, v2, ou
                         ident_f[:],
                     )
             w_dst = wgs[g][:, 1024 * q : 1024 * (q + 1)].bitcast(F32).rearrange("p (c u) -> p c u", u=2)
-            w_src = wt[:].rearrange("p u c -> p c u")
-            if q == 0:
-                nc.vector.tensor_copy(out=w_dst, in_=w_src)
-            else:
-                nc.scalar.copy(out=w_dst, in_=w_src)
+            nc.scalar.copy(out=w_dst, in_=wt[:].rearrange("p u c -> p c u"))
 
         def quant_w(h):
             for g in range(2):
@@ -174,50 +168,41 @@ def tile_full_tmix_params_pb_t_kernel(tc, x, v_first, x_v, Wv, v0, xv_v1, v2, ou
                     in_=wgs[g][:, 2048 * h : 2048 * (h + 1)],
                 )
 
-        half_xt = {}
+        head_xt = {}
 
-        def half_xtr(hh, u):
-            if hh == 0:
-                xt = psZ.tile([P, HALF], F32, name="xt", tag="zz")
-            else:
-                xt = psA.tile([P, HALF], F32, name="xt", tag="xt")
-            for tt in range(2):
+        def head_xtr(lo, hi, u, pool, tag):
+            xt = pool.tile([P, hi - lo], F32, name="xt", tag=tag)
+            for m in range(lo // P, hi // P):
                 nc.tensor.transpose(
-                    xt[:, P * tt : P * (tt + 1)],
-                    xs0[:, 2 * hh + tt, :].bitcast(F32)[:, u:256:2],
-                    ident_f[:],
+                    xt[:, P * m - lo : P * (m + 1) - lo], xs0[:, m, :].bitcast(F32)[:, u:256:2], ident_f[:]
                 )
-            half_xt[(hh, u)] = xt
+            head_xt[(lo, u)] = xt
 
-        def half_t2(hh, u):
-            if hh == 0 and u == 0:
+        def head_t2(lo, hi, u):
+            if lo == 0 and u == 0:
                 t2 = t2pool.tile([P, 4, TW], F32, name="t2")
                 t2_tiles[(0, 0)] = t2
                 nc.scalar.copy(out=t2[:, :, 0:1], in_=zero4[:].unsqueeze(2))
             t2 = t2_tiles[(0, 0)]
-            xb = half_xt[(hh, u)][:].bitcast(BF16).rearrange("p (t e) -> p t e", e=2)
+            xb = head_xt[(lo, u)][:].bitcast(BF16).rearrange("p (t e) -> p t e", e=2)
             for e in range(2):
                 j = 2 * u + e
                 nc.scalar.activation(
-                    out=t2[:, j, HALF * hh + 1 : HALF * (hh + 1) + 1],
-                    in_=xb[:, :, e],
-                    func=ACT.Copy,
-                    scale=w_col[:, j : j + 1],
+                    out=t2[:, j, lo + 1 : hi + 1], in_=xb[:, :, e], func=ACT.Copy, scale=w_col[:, j : j + 1]
                 )
 
-        def half_a2(hh, u):
-            if hh == 0 and u == 0:
+        def head_a2(lo, hi, u):
+            if lo == 0 and u == 0:
                 xvp = xvpool.tile([P, 4, CHUNK], BF16, name="xvp")
                 xvp_tiles[(0, 0)] = xvp
-            ts = slice(HALF * hh, HALF * (hh + 1))
-            xb = half_xt[(hh, u)][:].bitcast(BF16).rearrange("p (t e) -> p t e", e=2)
+            xb = head_xt[(lo, u)][:].bitcast(BF16).rearrange("p (t e) -> p t e", e=2)
             for e in range(2):
                 j = 2 * u + e
                 nc.vector.scalar_tensor_tensor(
-                    out=xvp_tiles[(0, 0)][:, j, ts],
+                    out=xvp_tiles[(0, 0)][:, j, lo:hi],
                     in0=xb[:, :, e],
                     scalar=omw[:, j : j + 1],
-                    in1=t2_tiles[(0, 0)][:, j, ts],
+                    in1=t2_tiles[(0, 0)][:, j, lo:hi],
                     op0=ALU.mult,
                     op1=ALU.add,
                 )
@@ -226,7 +211,10 @@ def tile_full_tmix_params_pb_t_kernel(tc, x, v_first, x_v, Wv, v0, xv_v1, v2, ou
             ck, i = divmod(a, 4)
             g, u = divmod(i, 2)
             xs = xs_tiles[ck]
-            xt = psA.tile([P, CHUNK], F32, name="xt")
+            if a == 2:
+                xt = psP.tile([P, CHUNK], F32, name="xt", tag="pp")
+            else:
+                xt = psA.tile([P, CHUNK], F32, name="xt", tag="xt")
             for tt in range(4):
                 nc.tensor.transpose(
                     xt[:, P * tt : P * (tt + 1)],
@@ -410,50 +398,56 @@ def tile_full_tmix_params_pb_t_kernel(tc, x, v_first, x_v, Wv, v0, xv_v1, v2, ou
                 cs = slice(lo, lo + 512)
                 nc.sync.dma_start(out=of[P * n : P * (n + 1), cs], in_=d[:, cs])
 
-        half_xtr(0, 0)
-        half_t2(0, 0)
-        half_xtr(0, 1)
-        half_t2(0, 1)
-        half_a2(0, 0)
-        half_xtr(1, 0)
-        half_t2(1, 0)
-        half_a2(0, 1)
-        half_xtr(1, 1)
-        half_t2(1, 1)
-        half_a2(1, 0)
+        head_xtr(0, 128, 0, psZ, "zz")
+        head_t2(0, 128, 0)
+        head_xtr(0, 128, 1, psZ, "zz")
+        head_t2(0, 128, 1)
+        head_a2(0, 128, 0)
+        head_xtr(128, 256, 0, psP, "pp")
+        head_t2(128, 256, 0)
+        head_a2(0, 128, 1)
+        head_xtr(128, 256, 1, psP, "pp")
+        head_t2(128, 256, 1)
+        head_a2(128, 256, 0)
+        head_xtr(256, 512, 0, psA, "xt")
+        head_t2(256, 512, 0)
+        head_a2(128, 256, 1)
+        head_xtr(256, 512, 1, psA, "xt")
+        head_t2(256, 512, 1)
+        head_a2(256, 512, 0)
         rg(0)
-        prep_w(0, 0)
         xtr(2)
         t2ops(2)
-        half_a2(1, 1)
-        prep_w(0, 1)
+        xtr(3)
+        head_a2(256, 512, 1)
         a2ops(2)
+        t2ops(3)
+        prep_w(0, 0)
+        prep_w(0, 1)
+        a2ops(3)
+        rg(1)
         prep_w(1, 0)
         prep_w(1, 1)
-        xtr(3)
-        t2ops(3)
-        prep_v0()
         prep_w(2, 0)
         prep_w(2, 1)
-        quant_w(0)
-        rg(1)
-        quanth(0)
-        a2ops(3)
         prep_w(3, 1)
         xtr(4)
         t2ops(4)
-        prep_aT(0)
-        prep_w(3, 0)
+        quanth(0)
+        quant_w(0)
         rg(2)
-        rg(3)
         quanth(1)
         a2ops(4)
+        prep_aT(0)
+        prep_v0()
+        rg(3)
+        prep_w(3, 0)
         quanth(2)
         xtr(5)
         t2ops(5)
-        quant_w(1)
         quanth(3)
         zgrp(0)
+        quant_w(1)
         load_vf(1)
         load_x(3, 1)
         for n in range(-1, NT + 1):
@@ -467,6 +461,8 @@ def tile_full_tmix_params_pb_t_kernel(tc, x, v_first, x_v, Wv, v0, xv_v1, v2, ou
                 load_vf((n + 9) // 4)
             if n + 7 < NT:
                 xtr(n + 7)
+            if n >= NT - 6 and n + 4 < NT:
+                rg(n + 4)
             if n + 1 < NT:
                 sig(n + 1)
             if (n + 3) % 4 == 0 and 1 <= (n + 3) // 4 < NCHUNK:
@@ -475,7 +471,7 @@ def tile_full_tmix_params_pb_t_kernel(tc, x, v_first, x_v, Wv, v0, xv_v1, v2, ou
                 mx(n + 1)
             if n + 2 < NT:
                 zgrp(n + 2)
-            if 4 <= n + 4 < NT:
+            if 4 <= n + 4 and n < NT - 6:
                 rg(n + 4)
             if n + 7 < NT:
                 t2ops(n + 7)

@@ -22,7 +22,7 @@ SEQ_CHUNKS = 1024 // CHUNK
 TW = CHUNK + 4
 HALF = CHUNK // 2
 HEAD_RG = 4
-GW = 224
+GW = 160
 GC = 1024 - GW
 
 FLOPS = 2 * TOK * C * C + 2 * TOK * DV * C

@@ -276,7 +276,9 @@ def tile_full_tmix_params_pb_t_kernel(tc, x, v_first, x_v, Wv, v0, xv_v1, v2, ou
             lo = HALF * hh
             dst = grp[:, lo : lo + HALF, :].rearrange("p (c i) j -> p c j i", i=4)
             src = xvp[:, :, lo : lo + HALF].rearrange("p j (c i) -> p c j i", i=4)
-            if r < HEAD_RG:
+            if r in (2, 3):
+                nc.vector.tensor_copy(out=dst, in_=src)
+            elif r < HEAD_RG:
                 nc.gpsimd.tensor_scalar(out=dst, in0=src, scalar1=1.0, scalar2=0.0, op0=ALU.mult, op1=ALU.add)
             else:
                 nc.scalar.copy(out=dst, in_=src)
@@ -420,33 +422,33 @@ def tile_full_tmix_params_pb_t_kernel(tc, x, v_first, x_v, Wv, v0, xv_v1, v2, ou
         t2ops(2)
         xtr(3)
         head_a2(256, 512, 1)
-        a2ops(2)
         t2ops(3)
         prep_w(0, 0)
         prep_w(0, 1)
-        a2ops(3)
-        rg(1)
+        a2ops(2)
         prep_w(1, 0)
         prep_w(1, 1)
+        a2ops(3)
+        rg(1)
+        rg(2)
         prep_w(2, 0)
         prep_w(2, 1)
         prep_w(3, 1)
+        quanth(0)
+        rg(3)
+        quanth(2)
         xtr(4)
         t2ops(4)
-        quanth(0)
-        quant_w(0)
-        rg(2)
-        quanth(1)
-        a2ops(4)
         prep_aT(0)
         prep_v0()
-        rg(3)
         prep_w(3, 0)
-        quanth(2)
         xtr(5)
-        t2ops(5)
+        quanth(1)
+        quant_w(0)
         quanth(3)
         zgrp(0)
+        t2ops(5)
+        a2ops(4)
         quant_w(1)
         load_vf(1)
         load_x(3, 1)

@@ -66,21 +66,26 @@ def tile_full_tmix_params_pb_t_kernel(tc, x, v_first, x_v, Wv, v0, xv_v1, v2, ou
         d_tiles = {}
         aT_tiles = {}
 
-        def load_x(ck, pieces):
+        def load_x(ck):
             xs = xpool.tile([P, 4, C], BF16, name="xs")
-            src = xf[CHUNK * ck : CHUNK * (ck + 1), :].rearrange("(t p) c -> p t c", p=P)
-            w = C // pieces
-            for i in range(pieces):
-                nc.sync.dma_start(out=xs[:, :, w * i : w * (i + 1)], in_=src[:, :, w * i : w * (i + 1)])
+            nc.sync.dma_start(
+                out=xs[:], in_=xf[CHUNK * ck : CHUNK * (ck + 1), :].rearrange("(t p) c -> p t c", p=P)
+            )
             xs_tiles[ck] = xs
 
-        def load_vf(ck):
+        def load_vf(ck, pieces):
             vt = vpool.tile([P, 4, C], BF16, name="vt")
-            nc.sync.dma_start(
-                out=vt[:],
-                in_=vff[CHUNK * ck : CHUNK * (ck + 1), :].rearrange("(t p) c -> p t c", p=P),
-            )
+            src = vff[CHUNK * ck : CHUNK * (ck + 1), :].rearrange("(t p) c -> p t c", p=P)
+            w = 4 // pieces
+            for lo in range(0, 4, w):
+                nc.sync.dma_start(out=vt[:, lo : lo + w, :], in_=src[:, lo : lo + w, :])
             vf_tiles[ck] = vt
+
+        a_sb = const.tile([P, NT, DV], BF16, name="a_sb")
+        a_view = af.rearrange("(m p) d -> p m d", p=P)
+
+        def load_a(ck):
+            nc.sync.dma_start(out=a_sb[:, 4 * ck : 4 * ck + 4, :], in_=a_view[:, 4 * ck : 4 * ck + 4, :])
 
         w_bf = const.tile([P, 2, 4], BF16, name="w_bf")
         nc.scalar.dma_start(out=w_bf[:], in_=x_v.rearrange("(g p j) -> p g j", g=2, j=4))
@@ -94,10 +99,11 @@ def tile_full_tmix_params_pb_t_kernel(tc, x, v_first, x_v, Wv, v0, xv_v1, v2, ou
         wv_view = Wv.rearrange("(o p) k -> p o k", p=P)
         for q in range(4):
             nc.sync.dma_start(out=wv_sb[:, 2 * q : 2 * q + 2, :], in_=wv_view[:, 2 * q : 2 * q + 2, :])
-        a_sb = const.tile([P, NT, DV], BF16, name="a_sb")
-        a_view = af.rearrange("(m p) d -> p m d", p=P)
-        load_x(1, 4)
-        nc.sync.dma_start(out=a_sb[:, 0:8, :], in_=a_view[:, 0:8, :])
+        xs1 = xpool.tile([P, 4, C], BF16, name="xs")
+        xs_tiles[1] = xs1
+        src1 = xf[CHUNK : 2 * CHUNK, :].rearrange("(t p) c -> p t c", p=P)
+        nc.sync.dma_start(out=xs1[:, :, 0:512], in_=src1[:, :, 0:512])
+        load_a(0)
         v0row = const.tile([P, P], BF16, name="v0row")
         nc.vector.memset(v0row[:], 0.0)
         nc.sync.dma_start(out=v0row[0:8, :], in_=v0.rearrange("(o p) -> o p", p=P))
@@ -106,9 +112,10 @@ def tile_full_tmix_params_pb_t_kernel(tc, x, v_first, x_v, Wv, v0, xv_v1, v2, ou
         nc.sync.dma_start(out=v0one[0:1, :], in_=v0.rearrange("(o c) -> o c", c=512)[0:1, :])
         v2_sb = const.tile([P, C], BF16, name="v2_sb")
         nc.sync.dma_start(out=v2_sb[:], in_=v2)
-        load_vf(0)
-        nc.sync.dma_start(out=a_sb[:, 8:NT, :], in_=a_view[:, 8:NT, :])
-        load_x(2, 1)
+        nc.sync.dma_start(out=xs1[:, :, 512:C], in_=src1[:, :, 512:C])
+        load_vf(0, 2)
+        load_x(2)
+        load_a(1)
 
         ident_f = const.tile([P, P], F32, name="ident_f")
         make_identity(nc, ident_f[:])
@@ -439,28 +446,29 @@ def tile_full_tmix_params_pb_t_kernel(tc, x, v_first, x_v, Wv, v0, xv_v1, v2, ou
         quanth(2)
         xtr(4)
         t2ops(4)
-        prep_aT(0)
         prep_v0()
+        prep_aT(0)
         prep_w(3, 0)
         xtr(5)
         quanth(1)
         quant_w(0)
         quanth(3)
-        zgrp(0)
         t2ops(5)
+        zgrp(0)
         a2ops(4)
         quant_w(1)
-        load_vf(1)
-        load_x(3, 1)
+        load_vf(1, 1)
+        load_x(3)
         for n in range(-1, NT + 1):
             if 0 <= n - 1 < NT:
                 fin(n - 1)
             if n == NT - 1:
                 last_v2op()
             if (n + 15) % 4 == 0 and 4 <= (n + 15) // 4 < NCHUNK:
-                load_x((n + 15) // 4, 1)
+                load_x((n + 15) // 4)
             if (n + 9) % 4 == 0 and 2 <= (n + 9) // 4 < NCHUNK:
-                load_vf((n + 9) // 4)
+                load_vf((n + 9) // 4, 1)
+                load_a((n + 9) // 4)
             if n + 7 < NT:
                 xtr(n + 7)
             if n >= NT - 6 and n + 4 < NT:

@@ -19,7 +19,7 @@ CHUNK = 512
 NCHUNK = TOK // CHUNK
 NT = TOK // P
 SEQ_CHUNKS = 1024 // CHUNK
-TW = CHUNK + 4
+TW = 2 * CHUNK + 4
 HALF = CHUNK // 2
 HEAD_RG = 4
 GW = 160
@@ -42,7 +42,6 @@ def tile_full_tmix_params_pb_t_kernel(tc, x, v_first, x_v, Wv, v0, xv_v1, v2, ou
         xpool = ctx.enter_context(tc.tile_pool(name="xpool", bufs=3))
         vpool = ctx.enter_context(tc.tile_pool(name="vpool", bufs=3))
         xvpool = ctx.enter_context(tc.tile_pool(name="xvpool", bufs=3))
-        t2pool = ctx.enter_context(tc.tile_pool(name="t2pool", bufs=3))
         gpool = ctx.enter_context(tc.tile_pool(name="gpool", bufs=2))
         cpool = ctx.enter_context(tc.tile_pool(name="cpool", bufs=4))
         spool = ctx.enter_context(tc.tile_pool(name="spool", bufs=3))
@@ -56,7 +55,6 @@ def tile_full_tmix_params_pb_t_kernel(tc, x, v_first, x_v, Wv, v0, xv_v1, v2, ou
         vf_tiles = {}
         xt_tiles = {}
         xvp_tiles = {}
-        t2_tiles = {}
         grp_tiles = {}
         xc_tiles = {}
         xsc_tiles = {}
@@ -123,10 +121,10 @@ def tile_full_tmix_params_pb_t_kernel(tc, x, v_first, x_v, Wv, v0, xv_v1, v2, ou
         make_identity(nc, ident_b[:])
         ones_b = const.tile([P, P], BF16, name="ones_b")
         nc.vector.memset(ones_b[:], 1.0)
-        zero4 = const.tile([P, 4], F32, name="zero4")
-        nc.vector.memset(zero4[:], 0.0)
+        zero1 = const.tile([P, 1], F32, name="zero1")
+        nc.vector.memset(zero1[:], 0.0)
         table_first = const.tile([P, 1], F32, name="table_first")
-        nc.scalar.activation(out=table_first[:], in_=zero4[:, 0:1], func=ACT.Sigmoid)
+        nc.scalar.activation(out=table_first[:], in_=zero1[:], func=ACT.Sigmoid)
 
         w_col = const.tile([P, 8], F32, name="w_col")
         nc.vector.tensor_copy(out=w_col[:], in_=w_bf[:].rearrange("p g j -> p (g j)"))
@@ -135,11 +133,25 @@ def tile_full_tmix_params_pb_t_kernel(tc, x, v_first, x_v, Wv, v0, xv_v1, v2, ou
             out=omw[:], in0=w_col[:], scalar1=-1.0, scalar2=1.0, op0=ALU.mult, op1=ALU.add
         )
         v0T = const.tile([P, 4, P], F32, name="v0T")
+        t2_0 = const.tile([P, 4, TW], F32, name="t2_0")
+        t2_1 = const.tile([P, 4, TW], F32, name="t2_1")
+        t2s = [t2_0, t2_1]
+        for t2 in t2s:
+            nc.vector.memset(t2[:, :, 0:1], 0.0)
+
+        sign = const.tile([P, 4], F32, name="sign")
+        nc.vector.memset(sign[:], 1.0)
+        nc.vector.memset(sign[:, 3:4], -1.0)
+        nc.vector.memset(sign[96:128, 2:3], -1.0)
 
         def prep_v0():
             v0ps = psZ.tile([P, P], BF16, name="v0ps", tag="zz")
             nc.tensor.transpose(v0ps[:], v0row[:], ident_b[:])
-            nc.scalar.copy(out=v0T[:], in_=v0ps[:, 4:8].unsqueeze(2).to_broadcast([P, 4, P]))
+            nc.scalar.copy(out=v0T[:, 0:2, :], in_=v0ps[:, 4:6].unsqueeze(2).to_broadcast([P, 2, P]))
+            for i in (2, 3):
+                nc.scalar.activation(
+                    out=v0T[:, i, :], in_=v0ps[:, 4 + i : 5 + i].to_broadcast([P, P]), func=ACT.Copy, scale=sign[:, i : i + 1]
+                )
 
         def prep_aT(ck):
             aps = psZ.tile([P, CHUNK], BF16, name="aps", tag="zz")
@@ -186,11 +198,7 @@ def tile_full_tmix_params_pb_t_kernel(tc, x, v_first, x_v, Wv, v0, xv_v1, v2, ou
             head_xt[(lo, u)] = xt
 
         def head_t2(lo, hi, u):
-            if lo == 0 and u == 0:
-                t2 = t2pool.tile([P, 4, TW], F32, name="t2")
-                t2_tiles[(0, 0)] = t2
-                nc.scalar.copy(out=t2[:, :, 0:1], in_=zero4[:].unsqueeze(2))
-            t2 = t2_tiles[(0, 0)]
+            t2 = t2s[0]
             xb = head_xt[(lo, u)][:].bitcast(BF16).rearrange("p (t e) -> p t e", e=2)
             for e in range(2):
                 j = 2 * u + e
@@ -209,7 +217,7 @@ def tile_full_tmix_params_pb_t_kernel(tc, x, v_first, x_v, Wv, v0, xv_v1, v2, ou
                     out=xvp_tiles[(0, 0)][:, j, lo:hi],
                     in0=xb[:, :, e],
                     scalar=omw[:, j : j + 1],
-                    in1=t2_tiles[(0, 0)][:, j, lo:hi],
+                    in1=t2s[0][:, j, lo:hi],
                     op0=ALU.mult,
                     op1=ALU.add,
                 )
@@ -233,22 +241,13 @@ def tile_full_tmix_params_pb_t_kernel(tc, x, v_first, x_v, Wv, v0, xv_v1, v2, ou
         def t2ops(a):
             ck, i = divmod(a, 4)
             g, u = divmod(i, 2)
-            if u == 0:
-                t2 = t2pool.tile([P, 4, TW], F32, name="t2")
-                t2_tiles[(ck, g)] = t2
-                if ck % SEQ_CHUNKS == 0:
-                    nc.scalar.copy(out=t2[:, :, 0:1], in_=zero4[:].unsqueeze(2))
-                else:
-                    nc.scalar.copy(
-                        out=t2[:, :, 0:1], in_=t2_tiles[(ck - 1, g)][:, :, CHUNK : CHUNK + 1]
-                    )
-            t2 = t2_tiles[(ck, g)]
+            lo = CHUNK * (ck % SEQ_CHUNKS)
             xb = xt_tiles[a][:].bitcast(BF16).rearrange("p (t e) -> p t e", e=2)
             for e in range(2):
                 j = 2 * u + e
                 pl = 4 * g + j
                 nc.scalar.activation(
-                    out=t2[:, j, 1 : CHUNK + 1], in_=xb[:, :, e], func=ACT.Copy, scale=w_col[:, pl : pl + 1]
+                    out=t2s[g][:, j, lo + 1 : lo + CHUNK + 1], in_=xb[:, :, e], func=ACT.Copy, scale=w_col[:, pl : pl + 1]
                 )
 
         def a2ops(a):
@@ -258,7 +257,7 @@ def tile_full_tmix_params_pb_t_kernel(tc, x, v_first, x_v, Wv, v0, xv_v1, v2, ou
                 xvp = xvpool.tile([P, 4, CHUNK], BF16, name="xvp")
                 xvp_tiles[(ck, g)] = xvp
             xvp = xvp_tiles[(ck, g)]
-            t2 = t2_tiles[(ck, g)]
+            lo = CHUNK * (ck % SEQ_CHUNKS)
             xb = xt_tiles[a][:].bitcast(BF16).rearrange("p (t e) -> p t e", e=2)
             for e in range(2):
                 j = 2 * u + e
@@ -267,7 +266,7 @@ def tile_full_tmix_params_pb_t_kernel(tc, x, v_first, x_v, Wv, v0, xv_v1, v2, ou
                     out=xvp[:, j, :],
                     in0=xb[:, :, e],
                     scalar=omw[:, pl : pl + 1],
-                    in1=t2[:, j, 0:CHUNK],
+                    in1=t2s[g][:, j, lo : lo + CHUNK],
                     op0=ALU.mult,
                     op1=ALU.add,
                 )
@@ -355,9 +354,9 @@ def tile_full_tmix_params_pb_t_kernel(tc, x, v_first, x_v, Wv, v0, xv_v1, v2, ou
             gs = spool.tile([P, C], F32, name="gs")
             gs_tiles[n] = gs
             if gp_ends(n):
-                parts = [(1, 512, GC, 1.0), (1, GC, C, -1.0), (0, 0, 512, 1.0)]
-            else:
                 parts = [(1, 512, C, 1.0), (0, 0, 512, 1.0)]
+            else:
+                parts = [(1, 512, GC, 1.0), (1, GC, C, -1.0), (0, 0, 512, 1.0)]
             for h, lo, hi, sign in parts:
                 nc.scalar.activation(
                     out=gs[:, lo:hi],
@@ -454,6 +453,9 @@ def tile_full_tmix_params_pb_t_kernel(tc, x, v_first, x_v, Wv, v0, xv_v1, v2, ou
         quant_w(0)
         quanth(3)
         t2ops(5)
+        nc.gpsimd.tensor_scalar(
+            out=v2_sb[:, GC:C], in0=v2_sb[:, GC:C], scalar1=-1.0, scalar2=0.0, op0=ALU.mult, op1=ALU.add
+        )
         zgrp(0)
         a2ops(4)
         quant_w(1)

from contextlib import ExitStack

import concourse.mybir as mybir
from concourse.masks import make_identity

F32 = mybir.dt.float32
BF16 = mybir.dt.bfloat16
U32 = mybir.dt.uint32
U8 = mybir.dt.uint8
FP8X4 = mybir.dt.float8_e4m3fn_x4
ALU = mybir.AluOpType
ACT = mybir.ActivationFunctionType

P = 128
TOK = 4096
C = 1024
DV = 128
CHUNK = 512
NCHUNK = TOK // CHUNK
NT = TOK // P
SEQ_CHUNKS = 1024 // CHUNK
TW = 2 * CHUNK + 4
HALF = CHUNK // 2
HEAD_RG = 4
GW = 160
GC = 1024 - GW

FLOPS = 2 * TOK * C * C + 2 * TOK * DV * C


def tile_full_tmix_params_pb_t_kernel(tc, x, v_first, x_v, Wv, v0, xv_v1, v2, out):
    nc = tc.nc
    xf = x.flatten_outer_dims()
    vff = v_first.flatten_outer_dims()
    af = xv_v1.flatten_outer_dims()
    of = out.flatten_outer_dims()

    with ExitStack() as ctx:
        ctx.enter_context(tc.manual_schedule())
        const = ctx.enter_context(tc.tile_pool(name="const", bufs=1))
        wpool = ctx.enter_context(tc.tile_pool(name="wpool", bufs=1))
        xpool = ctx.enter_context(tc.tile_pool(name="xpool", bufs=3))
        vpool = ctx.enter_context(tc.tile_pool(name="vpool", bufs=3))
        xvpool = ctx.enter_context(tc.tile_pool(name="xvpool", bufs=3))
        gpool = ctx.enter_context(tc.tile_pool(name="gpool", bufs=2))
        cpool = ctx.enter_context(tc.tile_pool(name="cpool", bufs=4))
        spool = ctx.enter_context(tc.tile_pool(name="spool", bufs=3))
        dpool = ctx.enter_context(tc.tile_pool(name="dpool", bufs=8))
        apool = ctx.enter_context(tc.tile_pool(name="apool", bufs=2))
        psA = ctx.enter_context(tc.psum_pool(name="psA", bufs=2))
        psP = ctx.enter_context(tc.psum_pool(name="psP", bufs=4))
        psZ = ctx.enter_context(tc.psum_pool(name="psZ", bufs=2))

        xs_tiles = {}
        vf_tiles = {}
        xt_tiles = {}
        xvp_tiles = {}
        grp_tiles = {}
        xc_tiles = {}
        xsc_tiles = {}
        pp_tiles = {}
        zz_tiles = {}
        gs_tiles = {}
        d_tiles = {}
        aT_tiles = {}

        def load_x(ck):
            xs = xpool.tile([P, 4, C], BF16, name="xs")
            nc.sync.dma_start(
                out=xs[:], in_=xf[CHUNK * ck : CHUNK * (ck + 1), :].rearrange("(t p) c -> p t c", p=P)
            )
            xs_tiles[ck] = xs

        def load_vf(ck, pieces):
            vt = vpool.tile([P, 4, C], BF16, name="vt")
            src = vff[CHUNK * ck : CHUNK * (ck + 1), :].rearrange("(t p) c -> p t c", p=P)
            w = 4 // pieces
            for lo in range(0, 4, w):
                nc.sync.dma_start(out=vt[:, lo : lo + w, :], in_=src[:, lo : lo + w, :])
            vf_tiles[ck] = vt

        a_sb = const.tile([P, NT, DV], BF16, name="a_sb")
        a_view = af.rearrange("(m p) d -> p m d", p=P)

        def load_a(ck):
            nc.sync.dma_start(out=a_sb[:, 4 * ck : 4 * ck + 4, :], in_=a_view[:, 4 * ck : 4 * ck + 4, :])

        w_bf = const.tile([P, 2, 4], BF16, name="w_bf")
        nc.scalar.dma_start(out=w_bf[:], in_=x_v.rearrange("(g p j) -> p g j", g=2, j=4))
        xs0 = xpool.tile([P, 4, C], BF16, name="xs")
        xs_tiles[0] = xs0
        src0 = xf[0:CHUNK, :].rearrange("(t p) c -> p t c", p=P)
        for lo, hi in ((0, 1), (1, 2), (2, 4)):
            nc.sync.dma_start(out=xs0[:, lo:hi, 0:512], in_=src0[:, lo:hi, 0:512])
        nc.sync.dma_start(out=xs0[:, :, 512:C], in_=src0[:, :, 512:C])
        wv_sb = wpool.tile([P, 8, C], BF16, name="wv_sb")
        wv_view = Wv.rearrange("(o p) k -> p o k", p=P)
        for q in range(4):
            nc.sync.dma_start(out=wv_sb[:, 2 * q : 2 * q + 2, :], in_=wv_view[:, 2 * q : 2 * q + 2, :])
        xs1 = xpool.tile([P, 4, C], BF16, name="xs")
        xs_tiles[1] = xs1
        src1 = xf[CHUNK : 2 * CHUNK, :].rearrange("(t p) c -> p t c", p=P)
        nc.sync.dma_start(out=xs1[:, :, 0:512], in_=src1[:, :, 0:512])
        load_a(0)
        v0row = const.tile([P, P], BF16, name="v0row")
        nc.vector.memset(v0row[:], 0.0)
        nc.sync.dma_start(out=v0row[0:8, :], in_=v0.rearrange("(o p) -> o p", p=P))
        v0one = const.tile([P, 512], BF16, name="v0one")
        nc.vector.memset(v0one[:], 0.0)
        nc.sync.dma_start(out=v0one[0:1, :], in_=v0.rearrange("(o c) -> o c", c=512)[0:1, :])
        v2_sb = const.tile([P, C], BF16, name="v2_sb")
        nc.sync.dma_start(out=v2_sb[:], in_=v2)
        nc.sync.dma_start(out=xs1[:, :, 512:C], in_=src1[:, :, 512:C])
        load_vf(0, 2)
        load_x(2)
        load_a(1)

        ident_f = const.tile([P, P], F32, name="ident_f")
        make_identity(nc, ident_f[:])
        ident_b = const.tile([P, P], BF16, name="ident_b")
        make_identity(nc, ident_b[:])
        ones_b = const.tile([P, P], BF16, name="ones_b")
        nc.vector.memset(ones_b[:], 1.0)
        zero1 = const.tile([P, 1], F32, name="zero1")
        nc.vector.memset(zero1[:], 0.0)
        table_first = const.tile([P, 1], F32, name="table_first")
        nc.scalar.activation(out=table_first[:], in_=zero1[:], func=ACT.Sigmoid)

        w_col = const.tile([P, 8], F32, name="w_col")
        nc.vector.tensor_copy(out=w_col[:], in_=w_bf[:].rearrange("p g j -> p (g j)"))
        omw = const.tile([P, 8], F32, name="omw")
        nc.vector.tensor_scalar(
            out=omw[:], in0=w_col[:], scalar1=-1.0, scalar2=1.0, op0=ALU.mult, op1=ALU.add
        )
        v0T = const.tile([P, 4, P], F32, name="v0T")
        t2_0 = const.tile([P, 4, TW], F32, name="t2_0")
        t2_1 = const.tile([P, 4, TW], F32, name="t2_1")
        t2s = [t2_0, t2_1]
        for t2 in t2s:
            nc.vector.memset(t2[:, :, 0:1], 0.0)

        sign = const.tile([P, 4], F32, name="sign")
        nc.vector.memset(sign[:], 1.0)
        nc.vector.memset(sign[:, 3:4], -1.0)
        nc.vector.memset(sign[96:128, 2:3], -1.0)

        def prep_v0():
            v0ps = psZ.tile([P, P], BF16, name="v0ps", tag="zz")
            nc.tensor.transpose(v0ps[:], v0row[:], ident_b[:])
            nc.scalar.copy(out=v0T[:, 0:2, :], in_=v0ps[:, 4:6].unsqueeze(2).to_broadcast([P, 2, P]))
            for i in (2, 3):
                nc.scalar.activation(
                    out=v0T[:, i, :], in_=v0ps[:, 4 + i : 5 + i].to_broadcast([P, P]), func=ACT.Copy, scale=sign[:, i : i + 1]
                )

        def prep_aT(ck):
            aps = psZ.tile([P, CHUNK], BF16, name="aps", tag="zz")
            for m in range(4):
                nc.tensor.transpose(aps[:, P * m : P * (m + 1)], a_sb[:, 4 * ck + m, :], ident_b[:])
            aT = apool.tile([P, CHUNK], BF16, name="aT")
            nc.scalar.copy(out=aT[:], in_=aps[:])
            aT_tiles[ck] = aT

        w_codes = const.tile([P, 2, C], U32, name="w_codes", align_bytes=64)
        w_scales = const.tile([P, 2, C], U8, name="w_scales", align_bytes=64)
        wg0 = wpool.tile([P, 4 * C], BF16, name="wg0", align_bytes=64)
        wg1 = wpool.tile([P, 4 * C], BF16, name="wg1", align_bytes=64)
        wgs = [wg0, wg1]

        def prep_w(q, g):
            wt = psP.tile([P, 2, 256], F32, name="wt", tag="pp")
            for u in range(2):
                for oo in range(2):
                    nc.tensor.transpose(
                        wt[:, u, P * oo : P * (oo + 1)],
                        wv_sb[:, 2 * q + oo, :].bitcast(F32)[:, 256 * g + u : 256 * (g + 1) : 2],
                        ident_f[:],
                    )
            w_dst = wgs[g][:, 1024 * q : 1024 * (q + 1)].bitcast(F32).rearrange("p (c u) -> p c u", u=2)
            nc.scalar.copy(out=w_dst, in_=wt[:].rearrange("p u c -> p c u"))

        def quant_w(h):
            for g in range(2):
                nc.vector.quantize_mx(
                    out=w_codes[:, g, 512 * h : 512 * (h + 1)].bitcast(FP8X4),
                    scales=w_scales[:, g, 512 * h : 512 * (h + 1)],
                    in_=wgs[g][:, 2048 * h : 2048 * (h + 1)],
                )

        head_xt = {}

        def head_xtr(lo, hi, u, pool, tag):
            xt = pool.tile([P, hi - lo], F32, name="xt", tag=tag)
            for m in range(lo // P, hi // P):
                nc.tensor.transpose(
                    xt[:, P * m - lo : P * (m + 1) - lo], xs0[:, m, :].bitcast(F32)[:, u:256:2], ident_f[:]
                )
            head_xt[(lo, u)] = xt

        def head_t2(lo, hi, u):
            t2 = t2s[0]
            xb = head_xt[(lo, u)][:].bitcast(BF16).rearrange("p (t e) -> p t e", e=2)
            for e in range(2):
                j = 2 * u + e
                nc.scalar.activation(
                    out=t2[:, j, lo + 1 : hi + 1], in_=xb[:, :, e], func=ACT.Copy, scale=w_col[:, j : j + 1]
                )

        def head_a2(lo, hi, u):
            if lo == 0 and u == 0:
                xvp = xvpool.tile([P, 4, CHUNK], BF16, name="xvp")
                xvp_tiles[(0, 0)] = xvp
            xb = head_xt[(lo, u)][:].bitcast(BF16).rearrange("p (t e) -> p t e", e=2)
            for e in range(2):
                j = 2 * u + e
                nc.vector.scalar_tensor_tensor(
                    out=xvp_tiles[(0, 0)][:, j, lo:hi],
                    in0=xb[:, :, e],
                    scalar=omw[:, j : j + 1],
                    in1=t2s[0][:, j, lo:hi],
                    op0=ALU.mult,
                    op1=ALU.add,
                )

        def xtr(a):
            ck, i = divmod(a, 4)
            g, u = divmod(i, 2)
            xs = xs_tiles[ck]
            if a == 2:
                xt = psP.tile([P, CHUNK], F32, name="xt", tag="pp")
            else:
                xt = psA.tile([P, CHUNK], F32, name="xt", tag="xt")
            for tt in range(4):
                nc.tensor.transpose(
                    xt[:, P * tt : P * (tt + 1)],
                    xs[:, tt, :].bitcast(F32)[:, 256 * g + u : 256 * (g + 1) : 2],
                    ident_f[:],
                )
            xt_tiles[a] = xt

        def t2ops(a):
            ck, i = divmod(a, 4)
            g, u = divmod(i, 2)
            lo = CHUNK * (ck % SEQ_CHUNKS)
            xb = xt_tiles[a][:].bitcast(BF16).rearrange("p (t e) -> p t e", e=2)
            for e in range(2):
                j = 2 * u + e
                pl = 4 * g + j
                nc.scalar.activation(
                    out=t2s[g][:, j, lo + 1 : lo + CHUNK + 1], in_=xb[:, :, e], func=ACT.Copy, scale=w_col[:, pl : pl + 1]
                )

        def a2ops(a):
            ck, i = divmod(a, 4)
            g, u = divmod(i, 2)
            if u == 0:
                xvp = xvpool.tile([P, 4, CHUNK], BF16, name="xvp")
                xvp_tiles[(ck, g)] = xvp
            xvp = xvp_tiles[(ck, g)]
            lo = CHUNK * (ck % SEQ_CHUNKS)
            xb = xt_tiles[a][:].bitcast(BF16).rearrange("p (t e) -> p t e", e=2)
            for e in range(2):
                j = 2 * u + e
                pl = 4 * g + j
                nc.vector.scalar_tensor_tensor(
                    out=xvp[:, j, :],
                    in0=xb[:, :, e],
                    scalar=omw[:, pl : pl + 1],
                    in1=t2s[g][:, j, lo : lo + CHUNK],
                    op0=ALU.mult,
                    op1=ALU.add,
                )

        def rg(r):
            ck, rr = divmod(r, 4)
            g, hh = divmod(rr, 2)
            if hh == 0:
                grp = gpool.tile([P, CHUNK, 4], BF16, name="grp", align_bytes=64)
                grp_tiles[(ck, g)] = grp
            grp = grp_tiles[(ck, g)]
            xvp = xvp_tiles[(ck, g)]
            lo = HALF * hh
            dst = grp[:, lo : lo + HALF, :].rearrange("p (c i) j -> p c j i", i=4)
            src = xvp[:, :, lo : lo + HALF].rearrange("p j (c i) -> p c j i", i=4)
            if r in (2, 3):
                nc.vector.tensor_copy(out=dst, in_=src)
            elif r < HEAD_RG:
                nc.gpsimd.tensor_scalar(out=dst, in0=src, scalar1=1.0, scalar2=0.0, op0=ALU.mult, op1=ALU.add)
            else:
                nc.scalar.copy(out=dst, in_=src)

        def quanth(r):
            ck, rr = divmod(r, 4)
            g, hh = divmod(rr, 2)
            if hh == 0:
                xc = cpool.tile([P, CHUNK], U32, name="xc", align_bytes=64)
                xsc = cpool.tile([P, CHUNK], U8, name="xsc", align_bytes=64)
                xc_tiles[(ck, g)] = xc
                xsc_tiles[(ck, g)] = xsc
            lo = HALF * hh
            nc.vector.quantize_mx(
                out=xc_tiles[(ck, g)][:, lo : lo + HALF].bitcast(FP8X4),
                scales=xsc_tiles[(ck, g)][:, lo : lo + HALF],
                in_=grp_tiles[(ck, g)][:, lo : lo + HALF, :].rearrange("p t j -> p (t j)"),
            )

        def mx(n):
            ck, tt = divmod(n, 4)
            ts = slice(P * tt, P * (tt + 1))
            for h in range(2):
                cs = slice(512 * h, 512 * (h + 1))
                if n >= NT - 5 and n % 3 == 0:
                    pp = psA.tile([P, 512], F32, name="pp", tag="xt")
                else:
                    pp = psP.tile([P, 512], F32, name="pp")
                pp_tiles[(n, h)] = pp
                for g in range(2):
                    nc.tensor.matmul_mx(
                        out=pp[:],
                        lhsT=xc_tiles[(ck, g)][:, ts].bitcast(FP8X4),
                        lhsT_scale=xsc_tiles[(ck, g)][:, ts],
                        rhs=w_codes[:, g, cs].bitcast(FP8X4),
                        rhs_scale=w_scales[:, g, cs],
                        start=(g == 0),
                        stop=(g == 1),
                    )

        def zgrp(n):
            ck, tt = divmod(n, 4)
            for h in (1, 0):
                cs = slice(512 * h, 512 * (h + 1))
                zz = psZ.tile([P, 512], F32, name="zz")
                zz_tiles[(n, h)] = zz
                if h == 0:
                    nc.tensor.matmul(out=zz[:], lhsT=ones_b[:], rhs=v0one[:], start=True, stop=False)
                else:
                    for i in range(4):
                        nc.tensor.matmul(
                            out=zz[:, P * i : P * (i + 1)],
                            lhsT=v0T[:, i, :],
                            rhs=ident_f[:],
                            is_transpose=True,
                            start=(i == 0),
                            stop=False,
                        )
                nc.tensor.matmul(
                    out=zz[:], lhsT=aT_tiles[ck][:, P * tt : P * (tt + 1)], rhs=v2_sb[:, cs], start=False, stop=True
                )

        def gp_ends(n):
            return n < NT - 6

        def sig(n):
            gs = spool.tile([P, C], F32, name="gs")
            gs_tiles[n] = gs
            if gp_ends(n):
                parts = [(1, 512, C, 1.0), (0, 0, 512, 1.0)]
            else:
                parts = [(1, 512, GC, 1.0), (1, GC, C, -1.0), (0, 0, 512, 1.0)]
            for h, lo, hi, sign in parts:
                nc.scalar.activation(
                    out=gs[:, lo:hi],
                    in_=zz_tiles[(n, h)][:, lo - 512 * h : hi - 512 * h],
                    func=ACT.Sigmoid,
                    scale=sign,
                )

        def v1(n):
            ck, tt = divmod(n, 4)
            d = dpool.tile([P, C], F32, name="d")
            d_tiles[n] = d
            for h in range(2):
                cs = slice(512 * h, 512 * (h + 1))
                nc.vector.tensor_tensor(
                    out=d[:, cs], in0=vf_tiles[ck][:, tt, cs], in1=pp_tiles[(n, h)][:], op=ALU.subtract
                )

        def v2op(n):
            d = d_tiles[n]
            if n < NT - 1:
                nc.gpsimd.tensor_tensor(out=d[:], in0=d[:], in1=gs_tiles[n][:], op=ALU.mult)
            else:
                nc.gpsimd.tensor_tensor(
                    out=d[:, 0:512], in0=d[:, 0:512], in1=gs_tiles[n][:, 0:512], op=ALU.mult
                )

        def last_v2op():
            d = d_tiles[NT - 1]
            nc.vector.tensor_tensor(
                out=d[:, 512:C], in0=d[:, 512:C], in1=gs_tiles[NT - 1][:, 512:C], op=ALU.mult
            )

        def gp_piece(n):
            ck, tt = divmod(n, 4)
            d = d_tiles[n]
            nc.gpsimd.tensor_tensor(out=d[:, GC:C], in0=vf_tiles[ck][:, tt, GC:C], in1=d[:, GC:C], op=ALU.subtract)

        def fin(n):
            d = d_tiles[n]
            for h in range(2):
                lo = 512 * h
                hi = GC if (h == 1 and gp_ends(n)) else lo + 512
                nc.vector.tensor_tensor(
                    out=d[:, lo:hi], in0=d[:, lo:hi], in1=pp_tiles[(n, h)][:, 0 : hi - lo], op=ALU.add
                )
                cs = slice(lo, lo + 512)
                nc.sync.dma_start(out=of[P * n : P * (n + 1), cs], in_=d[:, cs])

        head_xtr(0, 128, 0, psZ, "zz")
        head_t2(0, 128, 0)
        head_xtr(0, 128, 1, psZ, "zz")
        head_t2(0, 128, 1)
        head_a2(0, 128, 0)
        head_xtr(128, 256, 0, psP, "pp")
        head_t2(128, 256, 0)
        head_a2(0, 128, 1)
        head_xtr(128, 256, 1, psP, "pp")
        head_t2(128, 256, 1)
        head_a2(128, 256, 0)
        head_xtr(256, 512, 0, psA, "xt")
        head_t2(256, 512, 0)
        head_a2(128, 256, 1)
        head_xtr(256, 512, 1, psA, "xt")
        head_t2(256, 512, 1)
        head_a2(256, 512, 0)
        rg(0)
        xtr(2)
        t2ops(2)
        xtr(3)
        head_a2(256, 512, 1)
        t2ops(3)
        prep_w(0, 0)
        prep_w(0, 1)
        a2ops(2)
        prep_w(1, 0)
        prep_w(1, 1)
        a2ops(3)
        rg(1)
        rg(2)
        prep_w(2, 0)
        prep_w(2, 1)
        prep_w(3, 1)
        quanth(0)
        rg(3)
        quanth(2)
        xtr(4)
        t2ops(4)
        prep_v0()
        prep_aT(0)
        prep_w(3, 0)
        xtr(5)
        quanth(1)
        quant_w(0)
        quanth(3)
        t2ops(5)
        nc.gpsimd.tensor_scalar(
            out=v2_sb[:, GC:C], in0=v2_sb[:, GC:C], scalar1=-1.0, scalar2=0.0, op0=ALU.mult, op1=ALU.add
        )
        zgrp(0)
        a2ops(4)
        quant_w(1)
        load_vf(1, 1)
        load_x(3)
        for n in range(-1, NT + 1):
            if 0 <= n - 1 < NT:
                fin(n - 1)
            if n == NT - 1:
                last_v2op()
            if (n + 15) % 4 == 0 and 4 <= (n + 15) // 4 < NCHUNK:
                load_x((n + 15) // 4)
            if (n + 9) % 4 == 0 and 2 <= (n + 9) // 4 < NCHUNK:
                load_vf((n + 9) // 4, 1)
                load_a((n + 9) // 4)
            if n + 7 < NT:
                xtr(n + 7)
            if n >= NT - 6 and n + 4 < NT:
                rg(n + 4)
            if n + 1 < NT:
                sig(n + 1)
            if (n + 3) % 4 == 0 and 1 <= (n + 3) // 4 < NCHUNK:
                prep_aT((n + 3) // 4)
            if n + 1 < NT:
                mx(n + 1)
            if n + 2 < NT:
                zgrp(n + 2)
            if 4 <= n + 4 and n < NT - 6:
                rg(n + 4)
            if n + 7 < NT:
                t2ops(n + 7)
            if n + 6 < NT:
                a2ops(n + 6)
            if n + 1 < NT:
                v1(n + 1)
            if 4 <= n + 4 < NT:
                quanth(n + 4)
            if n + 1 < NT:
                v2op(n + 1)
            if n + 1 < NT and gp_ends(n + 1):
                gp_piece(n + 1)
